import numpy as np
import ml_dtypes


def mxq(x, axis, fmt="e4m3"):
    dtype, down = {"e4m3": (ml_dtypes.float8_e4m3fn, 7), "e5m2": (ml_dtypes.float8_e5m2, 14)}[fmt]
    v = np.moveaxis(np.asarray(x, np.float32).astype(ml_dtypes.bfloat16).astype(np.float64), axis, -1)
    blocks = v.reshape(v.shape[:-1] + (-1, 32))
    amax = np.abs(blocks).max(-1, keepdims=True)
    byte = np.maximum(np.where(amax > 0, np.frexp(amax)[1] - 1 + 127, 0) - down, 1)
    scale = np.exp2(byte - 127.0)
    codes = (blocks / scale).astype(np.float32).astype(dtype).astype(np.float64)
    return np.moveaxis((codes * scale).reshape(v.shape), -1, axis)


WIDE = False


def mx_kscale(k):
    if not WIDE:
        return np.ones(k)
    levels = np.array([10, -10, 5, -5, 0])
    if k % 512:
        return np.exp2(np.random.permutation(np.resize(levels, k // 32))).repeat(32)
    a = np.empty((k // 512, 16))
    for p in range(k // 512):
        a[p, :8] = np.random.permutation(np.resize(levels, 8))
        for g in range(8):
            far = levels[np.abs(levels - a[p, g]) >= 10]
            a[p, g + 8] = far[np.random.randint(len(far))]
    return np.exp2(a.ravel()).repeat(32)


BF16 = ml_dtypes.bfloat16


def bf(x):
    return np.asarray(x, np.float32).astype(BF16)


def f64(x):
    return np.asarray(x).astype(np.float64)


B, IN, H = 4096, 512, 512


def sigmoid(v):
    return 1.0 / (1.0 + np.exp(-v))


def setup_inputs():
    s, u = mx_kscale(IN), mx_kscale(H)
    return {'input': bf(np.random.standard_normal((B, IN)) * s),
            'state': bf(np.random.standard_normal((B, H)) * u),
            'W1': bf(np.random.standard_normal((IN, H)) * 0.7 / np.sqrt(IN) / s[:, None]),
            'W3': bf(np.random.standard_normal((IN, H)) * 0.7 / np.sqrt(IN) / s[:, None]),
            'U1': bf(np.random.standard_normal((H, H)) * 0.7 / np.sqrt(H) / u[:, None]),
            'U3': bf(np.random.standard_normal((H, H)) * 1.0 / np.sqrt(H) / u[:, None]),
            'bias_r': bf(np.random.standard_normal((1, H)) * 0.5),
            'bias_update': bf(np.random.standard_normal((1, H)) * 0.5)}


def reference(input, state, W1, W3, U1, U3, bias_r, bias_update):
    h = f64(state)
    xq = mxq(f64(input), 1, 'e4m3')
    hq = mxq(h, 1, 'e4m3')
    wComp1 = xq @ mxq(f64(W1), 0, 'e4m3')
    wComp3 = xq @ mxq(f64(W3), 0, 'e4m3')
    uComp1 = hq @ mxq(f64(U1), 0, 'e4m3')
    r = sigmoid(wComp1 + uComp1 + f64(bias_r))
    return np.tanh(wComp3 + (mxq(r * h, 1, 'e4m3') @ mxq(f64(U3), 0, 'e4m3')) + f64(bias_update))

@@ -1,0 +1,265 @@
+from contextlib import ExitStack
+
+import concourse.mybir as mybir
+from concourse.masks import make_identity
+
+F32 = mybir.dt.float32
+BF16 = mybir.dt.bfloat16
+U32 = mybir.dt.uint32
+U8 = mybir.dt.uint8
+FP8X4 = mybir.dt.float8_e4m3fn_x4
+ACT = mybir.ActivationFunctionType
+ALU = mybir.AluOpType
+
+P = 128
+PACK = 4
+ROWS = 4096
+FEAT = 512
+TILES = ROWS // P
+GROUP_TILES = 4
+GROUPS = TILES // GROUP_TILES
+GROUP_ROWS = GROUP_TILES * P
+CHUNKS = FEAT // P
+WORDS = FEAT // 2
+FLOPS = 4 * 2 * ROWS * FEAT * FEAT
+
+LEAD = 2
+LOADS_AHEAD = 5
+FIRST_FILLED = 2
+SINGLE_STORES = 2
+BANKS = {"transposes": 3, "gate": 3, "candidate": 2}
+TURNS = ("candidate",) * 2 + ("transposes",) * 3 + ("gate",) * 3
+
+
+def tile_grulrcell_pa_t_kernel(tc, x_in, h_in, w1, w3, u1, u3, bias_r, bias_u, out):
+    nc = tc.nc
+    with ExitStack() as ctx:
+        keep = ctx.enter_context(tc.tile_pool(name="keep", bufs=1))
+        work = ctx.enter_context(tc.tile_pool(name="work", bufs=2))
+        psum = {}
+        for role in BANKS:
+            psum[role] = ctx.enter_context(tc.psum_pool(name=role, bufs=BANKS[role]))
+        ctx.enter_context(tc.manual_schedule())
+
+        rows_of = {
+            "x": x_in.rearrange("(p t) k -> p t k", t=TILES),
+            "h": h_in.rearrange("(p t) k -> p t k", t=TILES),
+        }
+        out_rows = out.rearrange("(p t) n -> p t n", t=TILES)
+
+        w_loaded = {}
+        w_grouped = {}
+        w_codes = {}
+        w_scales = {}
+        loaded = {}
+        acts = {}
+        act_codes = {}
+        act_scales = {}
+        gates = {}
+        resets = {}
+        reset_codes = {}
+        reset_scales = {}
+        results = {}
+
+        def load_weight(key, src):
+            t = keep.tile([P, PACK, FEAT], BF16, name="w_loaded_" + key)
+            nc.sync.dma_start(out=t[:], in_=src.rearrange("(q t) n -> q t n", t=PACK))
+            w_loaded[key] = t
+
+        def load_rows(key, g, pieces=1):
+            t = work.tile([P, GROUP_TILES * FEAT], BF16, name="loaded_%s%d" % (key, g), tag="loaded_" + key,
+                          bufs=LOADS_AHEAD)
+            n = GROUP_TILES // pieces
+            for i in range(pieces):
+                nc.sync.dma_start(
+                    out=t[:, i * n * FEAT:(i + 1) * n * FEAT].rearrange("p (j k) -> p j k", j=n),
+                    in_=rows_of[key][:, g * GROUP_TILES + i * n:g * GROUP_TILES + (i + 1) * n, :],
+                )
+            loaded[(key, g)] = t
+
+        def regroup_weight(key, stationary):
+            grouped = work.tile([P, PACK * FEAT], BF16, name="w_grouped_" + key, tag="w_grouped", align_bytes=64)
+            if stationary:
+                src = w_loaded[key][:].rearrange("q t (m c) -> q c m t", c=CHUNKS)
+                dst = grouped[:].rearrange("q (c m t) -> q c m t", c=CHUNKS, t=PACK)
+                for half in range(2):
+                    pair = slice(2 * half, 2 * half + 2)
+                    nc.vector.tensor_copy(out=dst[:, pair], in_=src[:, pair])
+            else:
+                nc.vector.tensor_copy(
+                    out=grouped[:].rearrange("q (c i t) -> q c t i", i=4, t=PACK),
+                    in_=w_loaded[key][:].rearrange("q t (c i) -> q c t i", i=4),
+                )
+            w_grouped[key] = grouped
+
+        def quantise_weight(key, pieces):
+            codes = keep.tile([P, FEAT], U32, name="w_codes_" + key, align_bytes=64)
+            scales = keep.tile([P, FEAT], U8, name="w_scales_" + key, align_bytes=64)
+            n = FEAT // pieces
+            for i in range(pieces):
+                nc.vector.quantize_mx(
+                    out=codes[:, i * n:(i + 1) * n].bitcast(FP8X4),
+                    scales=scales[:, i * n:(i + 1) * n],
+                    in_=w_grouped[key][:, PACK * i * n:PACK * (i + 1) * n],
+                )
+            w_codes[key] = codes
+            w_scales[key] = scales
+
+        def transpose_group(g):
+            for key, bufs in (("x", LEAD + 1), ("h", LEAD + 2)):
+                src = loaded[(key, g)][:].bitcast(F32)
+                grouped = work.tile([P, PACK * GROUP_ROWS], BF16, name="acts_%s%d" % (key, g), tag="acts_" + key,
+                                    bufs=bufs, align_bytes=64)
+                words = grouped[:].bitcast(F32).rearrange("q (b r u) -> q b r u", b=2, u=2)
+                for b in range(2):
+                    bank = psum["transposes"].tile([P, 2, 2 * P], F32, name="t_%s%d_%d" % (key, g, b),
+                                                   tag="transposes")
+                    for j in range(2):
+                        first = (2 * b + j) * WORDS
+                        for u in range(2):
+                            nc.tensor.transpose(
+                                bank[:, u, j * P:(j + 1) * P],
+                                src[:, first + u:first + WORDS:2],
+                                identity[:],
+                            )
+                    nc.scalar.copy(out=words[:, b], in_=bank[:].rearrange("q u r -> q r u"))
+                acts[(key, g)] = grouped
+            for key in ("x", "h"):
+                if key == "x":
+                    codes = keep.tile([P, GROUP_ROWS], U32, name="x_codes%d" % g, align_bytes=64)
+                    scales = keep.tile([P, GROUP_ROWS], U8, name="x_scales%d" % g, align_bytes=64)
+                else:
+                    codes = work.tile([P, GROUP_ROWS], U32, name="h_codes%d" % g, tag="h_codes", bufs=LEAD + 1,
+                                      align_bytes=64)
+                    scales = work.tile([P, GROUP_ROWS], U8, name="h_scales%d" % g, tag="h_scales", bufs=LEAD + 1,
+                                       align_bytes=64)
+                nc.vector.quantize_mx(out=codes[:].bitcast(FP8X4), scales=scales[:], in_=acts[(key, g)][:])
+                act_codes[(key, g)] = codes
+                act_scales[(key, g)] = scales
+            if g + LOADS_AHEAD < GROUPS:
+                load_rows("x", g + LOADS_AHEAD)
+                load_rows("h", g + LOADS_AHEAD)
+
+        def gate(g):
+            r = work.tile([P, CHUNKS, GROUP_ROWS], F32, name="gate%d" % g, tag="gate")
+            for t in range(CHUNKS):
+                cols = slice(t * P, (t + 1) * P)
+                bank = psum["gate"].tile([P, GROUP_ROWS], F32, name="g_%d_%d" % (g, t), tag="gate")
+                for weight, key in (("w1", "x"), ("u1", "h")):
+                    nc.tensor.matmul_mx(
+                        out=bank[:],
+                        lhsT=w_codes[weight][:, cols].bitcast(FP8X4), lhsT_scale=w_scales[weight][:, cols],
+                        rhs=act_codes[(key, g)][:].bitcast(FP8X4), rhs_scale=act_scales[(key, g)][:],
+                        start=(key == "x"), stop=(key == "h"),
+                    )
+                nc.scalar.activation(out=r[:, t, :], in_=bank[:], func=ACT.Sigmoid, bias=bias_gate[:, t:t + 1],
+                                     scale=1.0)
+            gates[g] = r
+
+        def reset_state(g):
+            product = work.tile([P, PACK * GROUP_ROWS], BF16, name="reset%d" % g, tag="reset", align_bytes=64)
+            nc.vector.tensor_tensor(
+                out=product[:].rearrange("q (b i t) -> q b t i", i=4, t=PACK),
+                in0=gates[g][:].rearrange("q t (b i) -> q b t i", i=4),
+                in1=acts[("h", g)][:].rearrange("q (b i t) -> q b t i", i=4, t=PACK),
+                op=ALU.mult,
+            )
+            resets[g] = product
+
+        def quantise_reset_state(g):
+            codes = keep.tile([P, GROUP_ROWS], U32, name="reset_codes%d" % g, align_bytes=64)
+            scales = keep.tile([P, GROUP_ROWS], U8, name="reset_scales%d" % g, align_bytes=64)
+            nc.vector.quantize_mx(out=codes[:].bitcast(FP8X4), scales=scales[:], in_=resets[g][:])
+            reset_codes[g] = codes
+            reset_scales[g] = scales
+
+        def candidate_sum(i, role):
+            g, j = divmod(i, GROUP_TILES)
+            if j == 0:
+                results[g] = work.tile([P, GROUP_TILES, FEAT], F32, name="result%d" % g, tag="result", bufs=4)
+            rows = slice(j * P, (j + 1) * P)
+            bank = psum[role].tile([P, FEAT], F32, name="c_%d" % i, tag=role)
+            nc.tensor.matmul_mx(
+                out=bank[:],
+                lhsT=act_codes[("x", g)][:, rows].bitcast(FP8X4), lhsT_scale=act_scales[("x", g)][:, rows],
+                rhs=w_codes["w3"][:].bitcast(FP8X4), rhs_scale=w_scales["w3"][:],
+                start=True, stop=False,
+            )
+            nc.tensor.matmul_mx(
+                out=bank[:],
+                lhsT=reset_codes[g][:, rows].bitcast(FP8X4), lhsT_scale=reset_scales[g][:, rows],
+                rhs=w_codes["u3"][:].bitcast(FP8X4), rhs_scale=w_scales["u3"][:],
+                start=False, stop=True,
+            )
+            nc.vector.tensor_tensor(out=results[g][:, j, :], in0=bank[:], in1=bias_rows[:], op=ALU.add)
+
+        def finish(i):
+            g, j = divmod(i, GROUP_TILES)
+            result = results[g]
+            nc.scalar.activation(out=result[:, j, :], in_=result[:, j, :], func=ACT.Tanh)
+            if i >= TILES - SINGLE_STORES:
+                nc.sync.dma_start(out=out_rows[:, i:i + 1, :], in_=result[:, j:j + 1, :])
+            elif j % 2 == 1:
+                nc.sync.dma_start(out=out_rows[:, i - 1:i + 1, :], in_=result[:, j - 1:j + 1, :])
+
+        bias_gate_bf = keep.tile([P, CHUNKS], BF16, name="bias_gate_bf")
+        nc.scalar.dma_start(out=bias_gate_bf[:], in_=bias_r.rearrange("o (q t) -> q (o t)", t=CHUNKS))
+        bias_row = keep.tile([P, FEAT], BF16, name="bias_row")
+        nc.gpsimd.memset(bias_row[:], 0.0)
+        nc.scalar.dma_start(out=bias_row[0:1, :], in_=bias_u)
+        identity = keep.tile([P, P], F32, name="identity")
+        make_identity(nc, identity[:])
+        ones = keep.tile([P, P], BF16, name="ones")
+        nc.gpsimd.memset(ones[:], 1.0)
+        bias_rows = keep.tile([P, FEAT], F32, name="bias_rows")
+
+        load_weight("w1", w1)
+        load_rows("x", 0, pieces=2)
+        load_weight("u1", u1)
+        load_rows("h", 0, pieces=2)
+        load_rows("x", 1)
+        load_rows("h", 1)
+        load_weight("w3", w3)
+        load_weight("u3", u3)
+        for g in range(2, LOADS_AHEAD):
+            load_rows("x", g)
+            load_rows("h", g)
+
+        regroup_weight("w1", stationary=True)
+        quantise_weight("w1", pieces=2)
+        bias_gate = keep.tile([P, CHUNKS], F32, name="bias_gate")
+        nc.vector.tensor_copy(out=bias_gate[:], in_=bias_gate_bf[:])
+        regroup_weight("u1", stationary=True)
+        quantise_weight("u1", pieces=2)
+        for g in range(LEAD):
+            transpose_group(g)
+
+        filled = 0
+        for n in range(GROUPS):
+            gate(n)
+            if n == 0:
+                bank = psum["candidate"].tile([P, FEAT], F32, name="bias_bank", tag="candidate")
+                nc.tensor.matmul(out=bank[:], lhsT=ones[:], rhs=bias_row[:], start=True, stop=True)
+                nc.scalar.copy(out=bias_rows[:], in_=bank[:])
+                regroup_weight("w3", stationary=False)
+                regroup_weight("u3", stationary=False)
+                quantise_weight("w3", pieces=1)
+                quantise_weight("u3", pieces=1)
+            if n >= 1:
+                reset_state(n - 1)
+            if n >= FIRST_FILLED:
+                candidate_sum(filled, "candidate")
+                filled += 1
+            if n >= 1:
+                quantise_reset_state(n - 1)
+            if n + LEAD < GROUPS:
+                transpose_group(n + LEAD)
+
+        reset_state(GROUPS - 1)
+        for i in range(filled):
+            finish(i)
+        for i in range(filled, TILES):
+            candidate_sum(i, TURNS[(i - filled) % len(TURNS)])
+            if i == filled:
+                quantise_reset_state(GROUPS - 1)
+            finish(i)

@@ -105,8 +105,8 @@ def tile_grulrcell_pa_t_kernel(tc, x_in, h_in, w1, w3, u1, u3, bias_r, bias_u, o
             w_codes[key] = codes
             w_scales[key] = scales
 
-        def transpose_group(g):
-            for key, bufs in (("x", LEAD + 1), ("h", LEAD + 2)):
+        def transpose_rows(key, g):
+            for bufs in ({"x": LEAD + 1, "h": LEAD + 2}[key],):
                 src = loaded[(key, g)][:].bitcast(F32)
                 grouped = work.tile([P, PACK * GROUP_ROWS], BF16, name="acts_%s%d" % (key, g), tag="acts_" + key,
                                     bufs=bufs, align_bytes=64)
@@ -124,6 +124,8 @@ def tile_grulrcell_pa_t_kernel(tc, x_in, h_in, w1, w3, u1, u3, bias_r, bias_u, o
                             )
                     nc.scalar.copy(out=words[:, b], in_=bank[:].rearrange("q u r -> q r u"))
                 acts[(key, g)] = grouped
+
+        def quantise_rows(g):
             for key in ("x", "h"):
                 if key == "x":
                     codes = keep.tile([P, GROUP_ROWS], U32, name="x_codes%d" % g, align_bytes=64)
@@ -140,9 +142,11 @@ def tile_grulrcell_pa_t_kernel(tc, x_in, h_in, w1, w3, u1, u3, bias_r, bias_u, o
                 load_rows("x", g + LOADS_AHEAD)
                 load_rows("h", g + LOADS_AHEAD)
 
-        def gate(g):
-            r = work.tile([P, CHUNKS, GROUP_ROWS], F32, name="gate%d" % g, tag="gate")
-            for t in range(CHUNKS):
+        def gate(g, chunks):
+            if g not in gates:
+                gates[g] = work.tile([P, CHUNKS, GROUP_ROWS], F32, name="gate%d" % g, tag="gate")
+            r = gates[g]
+            for t in chunks:
                 cols = slice(t * P, (t + 1) * P)
                 bank = psum["gate"].tile([P, GROUP_ROWS], F32, name="g_%d_%d" % (g, t), tag="gate")
                 for weight, key in (("w1", "x"), ("u1", "h")):
@@ -154,7 +158,6 @@ def tile_grulrcell_pa_t_kernel(tc, x_in, h_in, w1, w3, u1, u3, bias_r, bias_u, o
                     )
                 nc.scalar.activation(out=r[:, t, :], in_=bank[:], func=ACT.Sigmoid, bias=bias_gate[:, t:t + 1],
                                      scale=1.0)
-            gates[g] = r
 
         def reset_state(g):
             product = work.tile([P, PACK * GROUP_ROWS], BF16, name="reset%d" % g, tag="reset", align_bytes=64)
@@ -232,11 +235,16 @@ def tile_grulrcell_pa_t_kernel(tc, x_in, h_in, w1, w3, u1, u3, bias_r, bias_u, o
         regroup_weight("u1", stationary=True)
         quantise_weight("u1", pieces=2)
         for g in range(LEAD):
-            transpose_group(g)
+            transpose_rows("x", g)
+            transpose_rows("h", g)
+            quantise_rows(g)
 
         filled = 0
         for n in range(GROUPS):
-            gate(n)
+            gate(n, (0, 1))
+            if n + LEAD < GROUPS:
+                transpose_rows("x", n + LEAD)
+            gate(n, (2, 3))
             if n == 0:
                 bank = psum["candidate"].tile([P, FEAT], F32, name="bias_bank", tag="candidate")
                 nc.tensor.matmul(out=bank[:], lhsT=ones[:], rhs=bias_row[:], start=True, stop=True)
@@ -253,7 +261,8 @@ def tile_grulrcell_pa_t_kernel(tc, x_in, h_in, w1, w3, u1, u3, bias_r, bias_u, o
             if n >= 1:
                 quantise_reset_state(n - 1)
             if n + LEAD < GROUPS:
-                transpose_group(n + LEAD)
+                transpose_rows("h", n + LEAD)
+                quantise_rows(n + LEAD)
 
         reset_state(GROUPS - 1)
         for i in range(filled):

@@ -27,6 +27,7 @@ LEAD = 2
 LOADS_AHEAD = 5
 FIRST_FILLED = 2
 SINGLE_STORES = 2
+ON_GPSIMD = 6
 BANKS = {"transposes": 3, "gate": 3, "candidate": 2}
 TURNS = ("candidate",) * 2 + ("transposes",) * 3 + ("gate",) * 3
 
@@ -159,14 +160,18 @@ def tile_grulrcell_pa_t_kernel(tc, x_in, h_in, w1, w3, u1, u3, bias_r, bias_u, o
                 nc.scalar.activation(out=r[:, t, :], in_=bank[:], func=ACT.Sigmoid, bias=bias_gate[:, t:t + 1],
                                      scale=1.0)
 
-        def reset_state(g):
+        def reset_state(g, engine, pieces):
             product = work.tile([P, PACK * GROUP_ROWS], BF16, name="reset%d" % g, tag="reset", align_bytes=64)
-            nc.vector.tensor_tensor(
-                out=product[:].rearrange("q (b i t) -> q b t i", i=4, t=PACK),
-                in0=gates[g][:].rearrange("q t (b i) -> q b t i", i=4),
-                in1=acts[("h", g)][:].rearrange("q (b i t) -> q b t i", i=4, t=PACK),
-                op=ALU.mult,
-            )
+            n = GROUP_ROWS // pieces
+            for j in range(pieces):
+                rows = slice(j * n, (j + 1) * n)
+                words = slice(PACK * j * n, PACK * (j + 1) * n)
+                engine.tensor_tensor(
+                    out=product[:, words].rearrange("q (b i t) -> q b t i", i=4, t=PACK),
+                    in0=gates[g][:, :, rows].rearrange("q t (b i) -> q b t i", i=4),
+                    in1=acts[("h", g)][:, words].rearrange("q (b i t) -> q b t i", i=4, t=PACK),
+                    op=ALU.mult,
+                )
             resets[g] = product
 
         def quantise_reset_state(g):
@@ -253,22 +258,25 @@ def tile_grulrcell_pa_t_kernel(tc, x_in, h_in, w1, w3, u1, u3, bias_r, bias_u, o
                 regroup_weight("u3", stationary=False)
                 quantise_weight("w3", pieces=1)
                 quantise_weight("u3", pieces=1)
-            if n >= 1:
-                reset_state(n - 1)
+            if 1 <= n <= ON_GPSIMD:
+                reset_state(n - 1, nc.vector, 1)
+            elif n > ON_GPSIMD:
+                reset_state(n - 1, nc.gpsimd, GROUP_TILES)
             if n >= FIRST_FILLED:
                 candidate_sum(filled, "candidate")
                 filled += 1
-            if n >= 1:
+            if 1 <= n <= ON_GPSIMD:
                 quantise_reset_state(n - 1)
             if n + LEAD < GROUPS:
                 transpose_rows("h", n + LEAD)
                 quantise_rows(n + LEAD)
 
-        reset_state(GROUPS - 1)
+        reset_state(GROUPS - 1, nc.gpsimd, GROUP_TILES)
         for i in range(filled):
             finish(i)
         for i in range(filled, TILES):
             candidate_sum(i, TURNS[(i - filled) % len(TURNS)])
-            if i == filled:
-                quantise_reset_state(GROUPS - 1)
+            if i % GROUP_TILES == 0 and i // GROUP_TILES + 2 >= ON_GPSIMD:
+                if i // GROUP_TILES + 2 < GROUPS:
+                    quantise_reset_state(i // GROUP_TILES + 2)
             finish(i)

@@ -29,7 +29,7 @@ FIRST_FILLED = 2
 SINGLE_STORES = 2
 ON_GPSIMD = 6
 BANKS = {"transposes": 3, "gate": 3, "candidate": 2}
-TURNS = ("candidate",) * 2 + ("transposes",) * 3 + ("gate",) * 3
+TURNS = ("transposes",) * 3 + ("candidate",) * 2 + ("gate",) * 3
 
 
 def tile_grulrcell_pa_t_kernel(tc, x_in, h_in, w1, w3, u1, u3, bias_r, bias_u, out):
@@ -245,6 +245,7 @@ def tile_grulrcell_pa_t_kernel(tc, x_in, h_in, w1, w3, u1, u3, bias_r, bias_u, o
             quantise_rows(g)
 
         filled = 0
+        finished = 0
         for n in range(GROUPS):
             gate(n, (0, 1))
             if n + LEAD < GROUPS:
@@ -270,9 +271,12 @@ def tile_grulrcell_pa_t_kernel(tc, x_in, h_in, w1, w3, u1, u3, bias_r, bias_u, o
             if n + LEAD < GROUPS:
                 transpose_rows("h", n + LEAD)
                 quantise_rows(n + LEAD)
+            else:
+                finish(finished)
+                finished += 1
 
         reset_state(GROUPS - 1, nc.gpsimd, GROUP_TILES)
-        for i in range(filled):
+        for i in range(finished, filled):
             finish(i)
         for i in range(filled, TILES):
             candidate_sum(i, TURNS[(i - filled) % len(TURNS)])

@@ -26,7 +26,6 @@ FLOPS = 4 * 2 * ROWS * FEAT * FEAT
 LEAD = 2
 LOADS_AHEAD = 5
 FIRST_FILLED = 2
-SINGLE_STORES = 2
 ON_GPSIMD = 6
 BANKS = {"transposes": 3, "gate": 3, "candidate": 2}
 TURNS = ("transposes",) * 3 + ("candidate",) * 2 + ("gate",) * 3
@@ -205,10 +204,7 @@ def tile_grulrcell_pa_t_kernel(tc, x_in, h_in, w1, w3, u1, u3, bias_r, bias_u, o
             g, j = divmod(i, GROUP_TILES)
             result = results[g]
             nc.scalar.activation(out=result[:, j, :], in_=result[:, j, :], func=ACT.Tanh)
-            if i >= TILES - SINGLE_STORES:
-                nc.sync.dma_start(out=out_rows[:, i:i + 1, :], in_=result[:, j:j + 1, :])
-            elif j % 2 == 1:
-                nc.sync.dma_start(out=out_rows[:, i - 1:i + 1, :], in_=result[:, j - 1:j + 1, :])
+            nc.sync.dma_start(out=out_rows[:, i:i + 1, :], in_=result[:, j:j + 1, :])
 
         bias_gate_bf = keep.tile([P, CHUNKS], BF16, name="bias_gate_bf")
         nc.scalar.dma_start(out=bias_gate_bf[:], in_=bias_r.rearrange("o (q t) -> q (o t)", t=CHUNKS))

@@ -78,7 +78,7 @@ def tile_grulrcell_pa_t_kernel(tc, x_in, h_in, w1, w3, u1, u3, bias_r, bias_u, o
             loaded[(key, g)] = t
 
         def regroup_weight(key, stationary):
-            grouped = work.tile([P, PACK * FEAT], BF16, name="w_grouped_" + key, tag="w_grouped", align_bytes=64)
+            grouped = work.tile([P, PACK * FEAT], BF16, name="w_grouped_" + key, tag="w_grouped", align_bytes=256)
             if stationary:
                 src = w_loaded[key][:].rearrange("q t (m c) -> q c m t", c=CHUNKS)
                 dst = grouped[:].rearrange("q (c m t) -> q c m t", c=CHUNKS, t=PACK)
@@ -93,8 +93,8 @@ def tile_grulrcell_pa_t_kernel(tc, x_in, h_in, w1, w3, u1, u3, bias_r, bias_u, o
             w_grouped[key] = grouped
 
         def quantise_weight(key, pieces):
-            codes = keep.tile([P, FEAT], U32, name="w_codes_" + key, align_bytes=64)
-            scales = keep.tile([P, FEAT], U8, name="w_scales_" + key, align_bytes=64)
+            codes = keep.tile([P, FEAT], U32, name="w_codes_" + key, align_bytes=256)
+            scales = keep.tile([P, FEAT], U8, name="w_scales_" + key, align_bytes=256)
             n = FEAT // pieces
             for i in range(pieces):
                 nc.vector.quantize_mx(
@@ -109,7 +109,7 @@ def tile_grulrcell_pa_t_kernel(tc, x_in, h_in, w1, w3, u1, u3, bias_r, bias_u, o
             for bufs in ({"x": LEAD + 1, "h": LEAD + 2}[key],):
                 src = loaded[(key, g)][:].bitcast(F32)
                 grouped = work.tile([P, PACK * GROUP_ROWS], BF16, name="acts_%s%d" % (key, g), tag="acts_" + key,
-                                    bufs=bufs, align_bytes=64)
+                                    bufs=bufs, align_bytes=256)
                 words = grouped[:].bitcast(F32).rearrange("q (b r u) -> q b r u", b=2, u=2)
                 for b in range(2):
                     bank = psum["transposes"].tile([P, 2, 2 * P], F32, name="t_%s%d_%d" % (key, g, b),
@@ -128,13 +128,13 @@ def tile_grulrcell_pa_t_kernel(tc, x_in, h_in, w1, w3, u1, u3, bias_r, bias_u, o
         def quantise_rows(g):
             for key in ("x", "h"):
                 if key == "x":
-                    codes = keep.tile([P, GROUP_ROWS], U32, name="x_codes%d" % g, align_bytes=64)
-                    scales = keep.tile([P, GROUP_ROWS], U8, name="x_scales%d" % g, align_bytes=64)
+                    codes = keep.tile([P, GROUP_ROWS], U32, name="x_codes%d" % g, align_bytes=256)
+                    scales = keep.tile([P, GROUP_ROWS], U8, name="x_scales%d" % g, align_bytes=256)
                 else:
                     codes = work.tile([P, GROUP_ROWS], U32, name="h_codes%d" % g, tag="h_codes", bufs=LEAD + 1,
-                                      align_bytes=64)
+                                      align_bytes=256)
                     scales = work.tile([P, GROUP_ROWS], U8, name="h_scales%d" % g, tag="h_scales", bufs=LEAD + 1,
-                                       align_bytes=64)
+                                       align_bytes=256)
                 nc.vector.quantize_mx(out=codes[:].bitcast(FP8X4), scales=scales[:], in_=acts[(key, g)][:])
                 act_codes[(key, g)] = codes
                 act_scales[(key, g)] = scales
@@ -160,7 +160,7 @@ def tile_grulrcell_pa_t_kernel(tc, x_in, h_in, w1, w3, u1, u3, bias_r, bias_u, o
                                      scale=1.0)
 
         def reset_state(g, engine, pieces):
-            product = work.tile([P, PACK * GROUP_ROWS], BF16, name="reset%d" % g, tag="reset", align_bytes=64)
+            product = work.tile([P, PACK * GROUP_ROWS], BF16, name="reset%d" % g, tag="reset", align_bytes=256)
             n = GROUP_ROWS // pieces
             for j in range(pieces):
                 rows = slice(j * n, (j + 1) * n)
@@ -174,8 +174,8 @@ def tile_grulrcell_pa_t_kernel(tc, x_in, h_in, w1, w3, u1, u3, bias_r, bias_u, o
             resets[g] = product
 
         def quantise_reset_state(g):
-            codes = keep.tile([P, GROUP_ROWS], U32, name="reset_codes%d" % g, align_bytes=64)
-            scales = keep.tile([P, GROUP_ROWS], U8, name="reset_scales%d" % g, align_bytes=64)
+            codes = keep.tile([P, GROUP_ROWS], U32, name="reset_codes%d" % g, align_bytes=256)
+            scales = keep.tile([P, GROUP_ROWS], U8, name="reset_scales%d" % g, align_bytes=256)
             nc.vector.quantize_mx(out=codes[:].bitcast(FP8X4), scales=scales[:], in_=resets[g][:])
             reset_codes[g] = codes
             reset_scales[g] = scales

@@ -25,7 +25,7 @@ FLOPS = 4 * 2 * ROWS * FEAT * FEAT
 
 LEAD = 2
 LOADS_AHEAD = 5
-FIRST_FILLED = 2
+FILLS = (0, 0, 1, 1, 1, 1, 2, 2)
 ON_GPSIMD = 6
 BANKS = {"transposes": 3, "gate": 3, "candidate": 2}
 TURNS = ("transposes",) * 3 + ("candidate",) * 2 + ("gate",) * 3
@@ -125,26 +125,24 @@ def tile_grulrcell_pa_t_kernel(tc, x_in, h_in, w1, w3, u1, u3, bias_r, bias_u, o
                     nc.scalar.copy(out=words[:, b], in_=bank[:].rearrange("q u r -> q r u"))
                 acts[(key, g)] = grouped
 
-        def quantise_rows(g):
-            for key in ("x", "h"):
-                if key == "x":
-                    codes = keep.tile([P, GROUP_ROWS], U32, name="x_codes%d" % g, align_bytes=256)
-                    scales = keep.tile([P, GROUP_ROWS], U8, name="x_scales%d" % g, align_bytes=256)
-                else:
-                    codes = work.tile([P, GROUP_ROWS], U32, name="h_codes%d" % g, tag="h_codes", bufs=LEAD + 1,
-                                      align_bytes=256)
-                    scales = work.tile([P, GROUP_ROWS], U8, name="h_scales%d" % g, tag="h_scales", bufs=LEAD + 1,
-                                       align_bytes=256)
-                nc.vector.quantize_mx(out=codes[:].bitcast(FP8X4), scales=scales[:], in_=acts[(key, g)][:])
-                act_codes[(key, g)] = codes
-                act_scales[(key, g)] = scales
+        def quantise_rows(key, g):
+            if key == "x":
+                codes = keep.tile([P, GROUP_ROWS], U32, name="x_codes%d" % g, align_bytes=256)
+                scales = keep.tile([P, GROUP_ROWS], U8, name="x_scales%d" % g, align_bytes=256)
+            else:
+                codes = work.tile([P, GROUP_ROWS], U32, name="h_codes%d" % g, tag="h_codes", bufs=LEAD + 1,
+                                  align_bytes=256)
+                scales = work.tile([P, GROUP_ROWS], U8, name="h_scales%d" % g, tag="h_scales", bufs=LEAD + 1,
+                                   align_bytes=256)
+            nc.vector.quantize_mx(out=codes[:].bitcast(FP8X4), scales=scales[:], in_=acts[(key, g)][:])
+            act_codes[(key, g)] = codes
+            act_scales[(key, g)] = scales
             if g + LOADS_AHEAD < GROUPS:
-                load_rows("x", g + LOADS_AHEAD)
-                load_rows("h", g + LOADS_AHEAD)
+                load_rows(key, g + LOADS_AHEAD)
 
         def gate(g, chunks):
             if g not in gates:
-                gates[g] = work.tile([P, CHUNKS, GROUP_ROWS], F32, name="gate%d" % g, tag="gate")
+                gates[g] = work.tile([P, CHUNKS, GROUP_ROWS], F32, name="gate%d" % g, tag="gate", bufs=3)
             r = gates[g]
             for t in chunks:
                 cols = slice(t * P, (t + 1) * P)
@@ -159,19 +157,18 @@ def tile_grulrcell_pa_t_kernel(tc, x_in, h_in, w1, w3, u1, u3, bias_r, bias_u, o
                 nc.scalar.activation(out=r[:, t, :], in_=bank[:], func=ACT.Sigmoid, bias=bias_gate[:, t:t + 1],
                                      scale=1.0)
 
-        def reset_state(g, engine, pieces):
-            product = work.tile([P, PACK * GROUP_ROWS], BF16, name="reset%d" % g, tag="reset", align_bytes=256)
+        def reset_state(g, engine, j, pieces):
+            if j == 0:
+                resets[g] = work.tile([P, PACK * GROUP_ROWS], BF16, name="reset%d" % g, tag="reset", align_bytes=256)
             n = GROUP_ROWS // pieces
-            for j in range(pieces):
-                rows = slice(j * n, (j + 1) * n)
-                words = slice(PACK * j * n, PACK * (j + 1) * n)
-                engine.tensor_tensor(
-                    out=product[:, words].rearrange("q (b i t) -> q b t i", i=4, t=PACK),
-                    in0=gates[g][:, :, rows].rearrange("q t (b i) -> q b t i", i=4),
-                    in1=acts[("h", g)][:, words].rearrange("q (b i t) -> q b t i", i=4, t=PACK),
-                    op=ALU.mult,
-                )
-            resets[g] = product
+            rows = slice(j * n, (j + 1) * n)
+            words = slice(PACK * j * n, PACK * (j + 1) * n)
+            engine.tensor_tensor(
+                out=resets[g][:, words].rearrange("q (b i t) -> q b t i", i=4, t=PACK),
+                in0=gates[g][:, :, rows].rearrange("q t (b i) -> q b t i", i=4),
+                in1=acts[("h", g)][:, words].rearrange("q (b i t) -> q b t i", i=4, t=PACK),
+                op=ALU.mult,
+            )
 
         def quantise_reset_state(g):
             codes = keep.tile([P, GROUP_ROWS], U32, name="reset_codes%d" % g, align_bytes=256)
@@ -238,45 +235,52 @@ def tile_grulrcell_pa_t_kernel(tc, x_in, h_in, w1, w3, u1, u3, bias_r, bias_u, o
         for g in range(LEAD):
             transpose_rows("x", g)
             transpose_rows("h", g)
-            quantise_rows(g)
+            quantise_rows("x", g)
+            quantise_rows("h", g)
 
         filled = 0
         finished = 0
+        state_waits = None
         for n in range(GROUPS):
-            gate(n, (0, 1))
-            if n + LEAD < GROUPS:
-                transpose_rows("x", n + LEAD)
-            gate(n, (2, 3))
-            if n == 0:
-                bank = psum["candidate"].tile([P, FEAT], F32, name="bias_bank", tag="candidate")
-                nc.tensor.matmul(out=bank[:], lhsT=ones[:], rhs=bias_row[:], start=True, stop=True)
-                nc.scalar.copy(out=bias_rows[:], in_=bank[:])
-                regroup_weight("w3", stationary=False)
-                regroup_weight("u3", stationary=False)
-                quantise_weight("w3", pieces=1)
-                quantise_weight("u3", pieces=1)
-            if 1 <= n <= ON_GPSIMD:
-                reset_state(n - 1, nc.vector, 1)
-            elif n > ON_GPSIMD:
-                reset_state(n - 1, nc.gpsimd, GROUP_TILES)
-            if n >= FIRST_FILLED:
-                candidate_sum(filled, "candidate")
-                filled += 1
-            if 1 <= n <= ON_GPSIMD:
-                quantise_reset_state(n - 1)
-            if n + LEAD < GROUPS:
-                transpose_rows("h", n + LEAD)
-                quantise_rows(n + LEAD)
-            else:
-                finish(finished)
-                finished += 1
+            for half in range(2):
+                gate(n, (2 * half, 2 * half + 1))
+                if n == 0 and half == 1:
+                    bank = psum["candidate"].tile([P, FEAT], F32, name="bias_bank", tag="candidate")
+                    nc.tensor.matmul(out=bank[:], lhsT=ones[:], rhs=bias_row[:], start=True, stop=True)
+                    nc.scalar.copy(out=bias_rows[:], in_=bank[:])
+                    regroup_weight("w3", stationary=False)
+                    regroup_weight("u3", stationary=False)
+                    quantise_weight("w3", pieces=1)
+                    quantise_weight("u3", pieces=1)
+                if 1 <= n <= ON_GPSIMD:
+                    reset_state(n - 1, nc.vector, half, 2)
+                elif n > ON_GPSIMD:
+                    for j in range(2 * half, 2 * half + 2):
+                        reset_state(n - 1, nc.gpsimd, j, GROUP_TILES)
+                ready = filled
+                if half < FILLS[n]:
+                    candidate_sum(filled, "candidate")
+                    filled += 1
+                while finished < ready:
+                    finish(finished)
+                    finished += 1
+                if n + LEAD < GROUPS:
+                    transpose_rows(("x", "h")[half], n + LEAD)
+                if half == 0 and state_waits is not None:
+                    quantise_rows("h", state_waits)
+                    state_waits = None
+                if half == 1:
+                    if n + LEAD < GROUPS:
+                        quantise_rows("x", n + LEAD)
+                        state_waits = n + LEAD
+                    if 1 <= n <= ON_GPSIMD:
+                        quantise_reset_state(n - 1)
 
-        reset_state(GROUPS - 1, nc.gpsimd, GROUP_TILES)
-        for i in range(finished, filled):
-            finish(i)
+        for j in range(GROUP_TILES):
+            reset_state(GROUPS - 1, nc.gpsimd, j, GROUP_TILES)
         for i in range(filled, TILES):
+            if i % GROUP_TILES == 0 and ON_GPSIMD <= i // GROUP_TILES + 1 < GROUPS:
+                quantise_reset_state(i // GROUP_TILES + 1)
             candidate_sum(i, TURNS[(i - filled) % len(TURNS)])
-            if i % GROUP_TILES == 0 and i // GROUP_TILES + 2 >= ON_GPSIMD:
-                if i // GROUP_TILES + 2 < GROUPS:
-                    quantise_reset_state(i // GROUP_TILES + 2)
-            finish(i)
+            finish(i - 1)
+        finish(TILES - 1)

@@ -55,6 +55,7 @@ def tile_grulrcell_pa_t_kernel(tc, x_in, h_in, w1, w3, u1, u3, bias_r, bias_u, o
         acts = {}
         act_codes = {}
         act_scales = {}
+        gate_banks = {}
         gates = {}
         resets = {}
         reset_codes = {}
@@ -140,22 +141,27 @@ def tile_grulrcell_pa_t_kernel(tc, x_in, h_in, w1, w3, u1, u3, bias_r, bias_u, o
             if g + LOADS_AHEAD < GROUPS:
                 load_rows(key, g + LOADS_AHEAD)
 
+        def gate_pass(g, t, weight, key):
+            cols = slice(t * P, (t + 1) * P)
+            if key == "x":
+                gate_banks[(g, t)] = psum["gate"].tile([P, GROUP_ROWS], F32, name="g_%d_%d" % (g, t), tag="gate")
+            nc.tensor.matmul_mx(
+                out=gate_banks[(g, t)][:],
+                lhsT=w_codes[weight][:, cols].bitcast(FP8X4), lhsT_scale=w_scales[weight][:, cols],
+                rhs=act_codes[(key, g)][:].bitcast(FP8X4), rhs_scale=act_scales[(key, g)][:],
+                start=(key == "x"), stop=(key == "h"),
+            )
+
         def gate(g, chunks):
             if g not in gates:
                 gates[g] = work.tile([P, CHUNKS, GROUP_ROWS], F32, name="gate%d" % g, tag="gate", bufs=3)
             r = gates[g]
             for t in chunks:
-                cols = slice(t * P, (t + 1) * P)
-                bank = psum["gate"].tile([P, GROUP_ROWS], F32, name="g_%d_%d" % (g, t), tag="gate")
-                for weight, key in (("w1", "x"), ("u1", "h")):
-                    nc.tensor.matmul_mx(
-                        out=bank[:],
-                        lhsT=w_codes[weight][:, cols].bitcast(FP8X4), lhsT_scale=w_scales[weight][:, cols],
-                        rhs=act_codes[(key, g)][:].bitcast(FP8X4), rhs_scale=act_scales[(key, g)][:],
-                        start=(key == "x"), stop=(key == "h"),
-                    )
-                nc.scalar.activation(out=r[:, t, :], in_=bank[:], func=ACT.Sigmoid, bias=bias_gate[:, t:t + 1],
-                                     scale=1.0)
+                if (g, t) not in gate_banks:
+                    gate_pass(g, t, "w1", "x")
+                gate_pass(g, t, "u1", "h")
+                nc.scalar.activation(out=r[:, t, :], in_=gate_banks[(g, t)][:], func=ACT.Sigmoid,
+                                     bias=bias_gate[:, t:t + 1], scale=1.0)
 
         def reset_state(g, engine, j, pieces):
             if j == 0:
@@ -216,27 +222,44 @@ def tile_grulrcell_pa_t_kernel(tc, x_in, h_in, w1, w3, u1, u3, bias_r, bias_u, o
 
         load_weight("w1", w1)
         load_rows("x", 0, pieces=2)
-        load_weight("u1", u1)
         load_rows("h", 0, pieces=2)
-        load_rows("x", 1)
-        load_rows("h", 1)
+        load_weight("u1", u1)
+        load_rows("x", 1, pieces=1)
+        load_rows("h", 1, pieces=1)
+        load_rows("x", 2, pieces=1)
+        load_rows("h", 2, pieces=1)
         load_weight("w3", w3)
         load_weight("u3", u3)
-        for g in range(2, LOADS_AHEAD):
-            load_rows("x", g)
-            load_rows("h", g)
+        load_rows("x", 3, pieces=1)
+        load_rows("h", 3, pieces=1)
+        load_rows("x", 4, pieces=1)
+        load_rows("h", 4, pieces=1)
 
+        zeros = keep.tile([P, FEAT], BF16, name="zeros")
+        nc.vector.memset(zeros[:], 0.0)
+
+        def keep_clock(name, matmuls):
+            bank = psum["gate"].tile([P, FEAT], F32, name=name, tag="gate")
+            for i in range(matmuls):
+                nc.tensor.matmul(out=bank[:], lhsT=zeros[:, :P], rhs=zeros[:], start=True, stop=True)
+
+        keep_clock("unread_a", 7)
+        transpose_rows("x", 0)
         regroup_weight("w1", stationary=True)
         quantise_weight("w1", pieces=2)
+        quantise_rows("x", 0)
+        keep_clock("unread_b", 2)
+        transpose_rows("h", 0)
         bias_gate = keep.tile([P, CHUNKS], F32, name="bias_gate")
         nc.vector.tensor_copy(out=bias_gate[:], in_=bias_gate_bf[:])
+        for t in range(3):
+            gate_pass(0, t, "w1", "x")
         regroup_weight("u1", stationary=True)
         quantise_weight("u1", pieces=2)
-        for g in range(LEAD):
-            transpose_rows("x", g)
-            transpose_rows("h", g)
-            quantise_rows("x", g)
-            quantise_rows("h", g)
+        quantise_rows("h", 0)
+        for key in ("x", "h"):
+            transpose_rows(key, 1)
+            quantise_rows(key, 1)
 
         filled = 0
         finished = 0

@@ -209,6 +209,10 @@ def tile_grulrcell_pa_t_kernel(tc, x_in, h_in, w1, w3, u1, u3, bias_r, bias_u, o
             nc.scalar.activation(out=result[:, j, :], in_=result[:, j, :], func=ACT.Tanh)
             nc.sync.dma_start(out=out_rows[:, i:i + 1, :], in_=result[:, j:j + 1, :])
 
+        first_sigmoid = keep.tile([P, 1], F32, name="first_sigmoid")
+        nc.vector.memset(first_sigmoid[:], 0.0)
+        nc.scalar.activation(out=first_sigmoid[:], in_=first_sigmoid[:], func=ACT.Sigmoid)
+
         bias_gate_bf = keep.tile([P, CHUNKS], BF16, name="bias_gate_bf")
         nc.scalar.dma_start(out=bias_gate_bf[:], in_=bias_r.rearrange("o (q t) -> q (o t)", t=CHUNKS))
         bias_row = keep.tile([P, FEAT], BF16, name="bias_row")

@@ -83,9 +83,7 @@ def tile_grulrcell_pa_t_kernel(tc, x_in, h_in, w1, w3, u1, u3, bias_r, bias_u, o
             if stationary:
                 src = w_loaded[key][:].rearrange("q t (m c) -> q c m t", c=CHUNKS)
                 dst = grouped[:].rearrange("q (c m t) -> q c m t", c=CHUNKS, t=PACK)
-                for half in range(2):
-                    pair = slice(2 * half, 2 * half + 2)
-                    nc.vector.tensor_copy(out=dst[:, pair], in_=src[:, pair])
+                nc.vector.tensor_copy(out=dst, in_=src)
             else:
                 nc.vector.tensor_copy(
                     out=grouped[:].rearrange("q (c i t) -> q c t i", i=4, t=PACK),
@@ -250,17 +248,17 @@ def tile_grulrcell_pa_t_kernel(tc, x_in, h_in, w1, w3, u1, u3, bias_r, bias_u, o
         keep_clock("unread_a", 7)
         transpose_rows("x", 0)
         regroup_weight("w1", stationary=True)
-        quantise_weight("w1", pieces=2)
+        bias_gate = keep.tile([P, CHUNKS], F32, name="bias_gate")
+        nc.vector.tensor_copy(out=bias_gate[:], in_=bias_gate_bf[:])
+        quantise_weight("w1", pieces=1)
         quantise_rows("x", 0)
         keep_clock("unread_b", 2)
         transpose_rows("h", 0)
-        bias_gate = keep.tile([P, CHUNKS], F32, name="bias_gate")
-        nc.vector.tensor_copy(out=bias_gate[:], in_=bias_gate_bf[:])
         for t in range(3):
             gate_pass(0, t, "w1", "x")
         regroup_weight("u1", stationary=True)
-        quantise_weight("u1", pieces=2)
         quantise_rows("h", 0)
+        quantise_weight("u1", pieces=1)
         for key in ("x", "h"):
             transpose_rows(key, 1)
             quantise_rows(key, 1)
@@ -280,7 +278,8 @@ def tile_grulrcell_pa_t_kernel(tc, x_in, h_in, w1, w3, u1, u3, bias_r, bias_u, o
                     quantise_weight("w3", pieces=1)
                     quantise_weight("u3", pieces=1)
                 if 1 <= n <= ON_GPSIMD:
-                    reset_state(n - 1, nc.vector, half, 2)
+                    if half == 0:
+                        reset_state(n - 1, nc.vector, 0, 1)
                 elif n > ON_GPSIMD:
                     for j in range(2 * half, 2 * half + 2):
                         reset_state(n - 1, nc.gpsimd, j, GROUP_TILES)
@@ -306,7 +305,7 @@ def tile_grulrcell_pa_t_kernel(tc, x_in, h_in, w1, w3, u1, u3, bias_r, bias_u, o
         for j in range(GROUP_TILES):
             reset_state(GROUPS - 1, nc.gpsimd, j, GROUP_TILES)
         for i in range(filled, TILES):
-            if i % GROUP_TILES == 0 and ON_GPSIMD <= i // GROUP_TILES + 1 < GROUPS:
+            if i % GROUP_TILES == 2 and ON_GPSIMD <= i // GROUP_TILES + 1 < GROUPS:
                 quantise_reset_state(i // GROUP_TILES + 1)
             candidate_sum(i, TURNS[(i - filled) % len(TURNS)])
             finish(i - 1)

@@ -27,6 +27,7 @@ LEAD = 2
 LOADS_AHEAD = 5
 FILLS = (0, 0, 1, 1, 1, 1, 2, 2)
 ON_GPSIMD = 6
+VECTOR_COPIES = 6
 BANKS = {"transposes": 3, "gate": 3, "candidate": 2}
 TURNS = ("transposes",) * 3 + ("candidate",) * 2 + ("gate",) * 3
 
@@ -121,7 +122,10 @@ def tile_grulrcell_pa_t_kernel(tc, x_in, h_in, w1, w3, u1, u3, bias_r, bias_u, o
                                 src[:, first + u:first + WORDS:2],
                                 identity[:],
                             )
-                    nc.scalar.copy(out=words[:, b], in_=bank[:].rearrange("q u r -> q r u"))
+                    if key == "x" and b == 0 and g == VECTOR_COPIES:
+                        nc.vector.tensor_copy(out=words[:, b], in_=bank[:].rearrange("q u r -> q r u"))
+                    else:
+                        nc.scalar.copy(out=words[:, b], in_=bank[:].rearrange("q u r -> q r u"))
                 acts[(key, g)] = grouped
 
         def quantise_rows(key, g):
@@ -181,6 +185,8 @@ def tile_grulrcell_pa_t_kernel(tc, x_in, h_in, w1, w3, u1, u3, bias_r, bias_u, o
             reset_codes[g] = codes
             reset_scales[g] = scales
 
+        cand_bank = {}
+
         def candidate_sum(i, role):
             g, j = divmod(i, GROUP_TILES)
             if j == 0:
@@ -199,7 +205,11 @@ def tile_grulrcell_pa_t_kernel(tc, x_in, h_in, w1, w3, u1, u3, bias_r, bias_u, o
                 rhs=w_codes["u3"][:].bitcast(FP8X4), rhs_scale=w_scales["u3"][:],
                 start=False, stop=True,
             )
-            nc.vector.tensor_tensor(out=results[g][:, j, :], in0=bank[:], in1=bias_rows[:], op=ALU.add)
+            cand_bank[i] = bank
+
+        def add_bias(i):
+            g, j = divmod(i, GROUP_TILES)
+            nc.vector.tensor_tensor(out=results[g][:, j, :], in0=cand_bank[i][:], in1=bias_rows[:], op=ALU.add)
 
         def finish(i):
             g, j = divmod(i, GROUP_TILES)
@@ -228,9 +238,9 @@ def tile_grulrcell_pa_t_kernel(tc, x_in, h_in, w1, w3, u1, u3, bias_r, bias_u, o
         load_weight("u1", u1)
         load_rows("x", 1, pieces=1)
         load_rows("h", 1, pieces=1)
+        load_weight("w3", w3)
         load_rows("x", 2, pieces=1)
         load_rows("h", 2, pieces=1)
-        load_weight("w3", w3)
         load_weight("u3", u3)
         load_rows("x", 3, pieces=1)
         load_rows("h", 3, pieces=1)
@@ -268,6 +278,8 @@ def tile_grulrcell_pa_t_kernel(tc, x_in, h_in, w1, w3, u1, u3, bias_r, bias_u, o
         state_waits = None
         for n in range(GROUPS):
             for half in range(2):
+                ready = filled
+                fill = half < FILLS[n]
                 gate(n, (2 * half, 2 * half + 1))
                 if n == 0 and half == 1:
                     bank = psum["candidate"].tile([P, FEAT], F32, name="bias_bank", tag="candidate")
@@ -283,8 +295,7 @@ def tile_grulrcell_pa_t_kernel(tc, x_in, h_in, w1, w3, u1, u3, bias_r, bias_u, o
                 elif n > ON_GPSIMD:
                     for j in range(2 * half, 2 * half + 2):
                         reset_state(n - 1, nc.gpsimd, j, GROUP_TILES)
-                ready = filled
-                if half < FILLS[n]:
+                if fill:
                     candidate_sum(filled, "candidate")
                     filled += 1
                 while finished < ready:
@@ -301,6 +312,8 @@ def tile_grulrcell_pa_t_kernel(tc, x_in, h_in, w1, w3, u1, u3, bias_r, bias_u, o
                         state_waits = n + LEAD
                     if 1 <= n <= ON_GPSIMD:
                         quantise_reset_state(n - 1)
+                if fill:
+                    add_bias(filled - 1)
 
         for j in range(GROUP_TILES):
             reset_state(GROUPS - 1, nc.gpsimd, j, GROUP_TILES)
@@ -308,5 +321,6 @@ def tile_grulrcell_pa_t_kernel(tc, x_in, h_in, w1, w3, u1, u3, bias_r, bias_u, o
             if i % GROUP_TILES == 2 and ON_GPSIMD <= i // GROUP_TILES + 1 < GROUPS:
                 quantise_reset_state(i // GROUP_TILES + 1)
             candidate_sum(i, TURNS[(i - filled) % len(TURNS)])
+            add_bias(i)
             finish(i - 1)
         finish(TILES - 1)

from contextlib import ExitStack

import concourse.mybir as mybir
from concourse.masks import make_identity

F32 = mybir.dt.float32
BF16 = mybir.dt.bfloat16
U32 = mybir.dt.uint32
U8 = mybir.dt.uint8
FP8X4 = mybir.dt.float8_e4m3fn_x4
ACT = mybir.ActivationFunctionType
ALU = mybir.AluOpType

P = 128
PACK = 4
ROWS = 4096
FEAT = 512
TILES = ROWS // P
GROUP_TILES = 4
GROUPS = TILES // GROUP_TILES
GROUP_ROWS = GROUP_TILES * P
CHUNKS = FEAT // P
WORDS = FEAT // 2
FLOPS = 4 * 2 * ROWS * FEAT * FEAT

LEAD = 2
LOADS_AHEAD = 5
FILLS = (0, 0, 1, 1, 1, 1, 2, 2)
ON_GPSIMD = 6
VECTOR_COPIES = 6
BANKS = {"transposes": 3, "gate": 3, "candidate": 2}
TURNS = ("transposes",) * 3 + ("candidate",) * 2 + ("gate",) * 3


def tile_grulrcell_pa_t_kernel(tc, x_in, h_in, w1, w3, u1, u3, bias_r, bias_u, out):
    nc = tc.nc
    with ExitStack() as ctx:
        keep = ctx.enter_context(tc.tile_pool(name="keep", bufs=1))
        work = ctx.enter_context(tc.tile_pool(name="work", bufs=2))
        psum = {}
        for role in BANKS:
            psum[role] = ctx.enter_context(tc.psum_pool(name=role, bufs=BANKS[role]))
        ctx.enter_context(tc.manual_schedule())

        rows_of = {
            "x": x_in.rearrange("(p t) k -> p t k", t=TILES),
            "h": h_in.rearrange("(p t) k -> p t k", t=TILES),
        }
        out_rows = out.rearrange("(p t) n -> p t n", t=TILES)

        w_loaded = {}
        w_grouped = {}
        w_codes = {}
        w_scales = {}
        loaded = {}
        acts = {}
        act_codes = {}
        act_scales = {}
        gate_banks = {}
        gates = {}
        resets = {}
        reset_codes = {}
        reset_scales = {}
        results = {}

        def load_weight(key, src):
            t = keep.tile([P, PACK, FEAT], BF16, name="w_loaded_" + key)
            nc.sync.dma_start(out=t[:], in_=src.rearrange("(q t) n -> q t n", t=PACK))
            w_loaded[key] = t

        def load_rows(key, g, pieces=1):
            t = work.tile([P, GROUP_TILES * FEAT], BF16, name="loaded_%s%d" % (key, g), tag="loaded_" + key,
                          bufs=LOADS_AHEAD)
            n = GROUP_TILES // pieces
            for i in range(pieces):
                nc.sync.dma_start(
                    out=t[:, i * n * FEAT:(i + 1) * n * FEAT].rearrange("p (j k) -> p j k", j=n),
                    in_=rows_of[key][:, g * GROUP_TILES + i * n:g * GROUP_TILES + (i + 1) * n, :],
                )
            loaded[(key, g)] = t

        def regroup_weight(key, stationary):
            grouped = work.tile([P, PACK * FEAT], BF16, name="w_grouped_" + key, tag="w_grouped", align_bytes=256)
            if stationary:
                src = w_loaded[key][:].rearrange("q t (m c) -> q c m t", c=CHUNKS)
                dst = grouped[:].rearrange("q (c m t) -> q c m t", c=CHUNKS, t=PACK)
                nc.vector.tensor_copy(out=dst, in_=src)
            else:
                nc.vector.tensor_copy(
                    out=grouped[:].rearrange("q (c i t) -> q c t i", i=4, t=PACK),
                    in_=w_loaded[key][:].rearrange("q t (c i) -> q c t i", i=4),
                )
            w_grouped[key] = grouped

        def quantise_weight(key, pieces):
            codes = keep.tile([P, FEAT], U32, name="w_codes_" + key, align_bytes=256)
            scales = keep.tile([P, FEAT], U8, name="w_scales_" + key, align_bytes=256)
            n = FEAT // pieces
            for i in range(pieces):
                nc.vector.quantize_mx(
                    out=codes[:, i * n:(i + 1) * n].bitcast(FP8X4),
                    scales=scales[:, i * n:(i + 1) * n],
                    in_=w_grouped[key][:, PACK * i * n:PACK * (i + 1) * n],
                )
            w_codes[key] = codes
            w_scales[key] = scales

        def transpose_rows(key, g):
            for bufs in ({"x": LEAD + 1, "h": LEAD + 2}[key],):
                src = loaded[(key, g)][:].bitcast(F32)
                grouped = work.tile([P, PACK * GROUP_ROWS], BF16, name="acts_%s%d" % (key, g), tag="acts_" + key,
                                    bufs=bufs, align_bytes=256)
                words = grouped[:].bitcast(F32).rearrange("q (b r u) -> q b r u", b=2, u=2)
                for b in range(2):
                    bank = psum["transposes"].tile([P, 2, 2 * P], F32, name="t_%s%d_%d" % (key, g, b),
                                                   tag="transposes")
                    for j in range(2):
                        first = (2 * b + j) * WORDS
                        for u in range(2):
                            nc.tensor.transpose(
                                bank[:, u, j * P:(j + 1) * P],
                                src[:, first + u:first + WORDS:2],
                                identity[:],
                            )
                    if key == "x" and b == 0 and g == VECTOR_COPIES:
                        nc.vector.tensor_copy(out=words[:, b], in_=bank[:].rearrange("q u r -> q r u"))
                    else:
                        nc.scalar.copy(out=words[:, b], in_=bank[:].rearrange("q u r -> q r u"))
                acts[(key, g)] = grouped

        def quantise_rows(key, g):
            if key == "x":
                codes = keep.tile([P, GROUP_ROWS], U32, name="x_codes%d" % g, align_bytes=256)
                scales = keep.tile([P, GROUP_ROWS], U8, name="x_scales%d" % g, align_bytes=256)
            else:
                codes = work.tile([P, GROUP_ROWS], U32, name="h_codes%d" % g, tag="h_codes", bufs=LEAD + 1,
                                  align_bytes=256)
                scales = work.tile([P, GROUP_ROWS], U8, name="h_scales%d" % g, tag="h_scales", bufs=LEAD + 1,
                                   align_bytes=256)
            nc.vector.quantize_mx(out=codes[:].bitcast(FP8X4), scales=scales[:], in_=acts[(key, g)][:])
            act_codes[(key, g)] = codes
            act_scales[(key, g)] = scales
            if g + LOADS_AHEAD < GROUPS:
                load_rows(key, g + LOADS_AHEAD)

        def gate_pass(g, t, weight, key):
            cols = slice(t * P, (t + 1) * P)
            if key == "x":
                gate_banks[(g, t)] = psum["gate"].tile([P, GROUP_ROWS], F32, name="g_%d_%d" % (g, t), tag="gate")
            nc.tensor.matmul_mx(
                out=gate_banks[(g, t)][:],
                lhsT=w_codes[weight][:, cols].bitcast(FP8X4), lhsT_scale=w_scales[weight][:, cols],
                rhs=act_codes[(key, g)][:].bitcast(FP8X4), rhs_scale=act_scales[(key, g)][:],
                start=(key == "x"), stop=(key == "h"),
            )

        def gate(g, chunks):
            if g not in gates:
                gates[g] = work.tile([P, CHUNKS, GROUP_ROWS], F32, name="gate%d" % g, tag="gate", bufs=3)
            r = gates[g]
            for t in chunks:
                if (g, t) not in gate_banks:
                    gate_pass(g, t, "w1", "x")
                gate_pass(g, t, "u1", "h")
                nc.scalar.activation(out=r[:, t, :], in_=gate_banks[(g, t)][:], func=ACT.Sigmoid,
                                     bias=bias_gate[:, t:t + 1], scale=1.0)

        def reset_state(g, engine, j, pieces):
            if j == 0:
                resets[g] = work.tile([P, PACK * GROUP_ROWS], BF16, name="reset%d" % g, tag="reset", align_bytes=256)
            n = GROUP_ROWS // pieces
            rows = slice(j * n, (j + 1) * n)
            words = slice(PACK * j * n, PACK * (j + 1) * n)
            engine.tensor_tensor(
                out=resets[g][:, words].rearrange("q (b i t) -> q b t i", i=4, t=PACK),
                in0=gates[g][:, :, rows].rearrange("q t (b i) -> q b t i", i=4),
                in1=acts[("h", g)][:, words].rearrange("q (b i t) -> q b t i", i=4, t=PACK),
                op=ALU.mult,
            )

        def quantise_reset_state(g):
            codes = keep.tile([P, GROUP_ROWS], U32, name="reset_codes%d" % g, align_bytes=256)
            scales = keep.tile([P, GROUP_ROWS], U8, name="reset_scales%d" % g, align_bytes=256)
            nc.vector.quantize_mx(out=codes[:].bitcast(FP8X4), scales=scales[:], in_=resets[g][:])
            reset_codes[g] = codes
            reset_scales[g] = scales

        cand_bank = {}

        def candidate_sum(i, role):
            g, j = divmod(i, GROUP_TILES)
            if j == 0:
                results[g] = work.tile([P, GROUP_TILES, FEAT], F32, name="result%d" % g, tag="result", bufs=4)
            rows = slice(j * P, (j + 1) * P)
            bank = psum[role].tile([P, FEAT], F32, name="c_%d" % i, tag=role)
            nc.tensor.matmul_mx(
                out=bank[:],
                lhsT=act_codes[("x", g)][:, rows].bitcast(FP8X4), lhsT_scale=act_scales[("x", g)][:, rows],
                rhs=w_codes["w3"][:].bitcast(FP8X4), rhs_scale=w_scales["w3"][:],
                start=True, stop=False,
            )
            nc.tensor.matmul_mx(
                out=bank[:],
                lhsT=reset_codes[g][:, rows].bitcast(FP8X4), lhsT_scale=reset_scales[g][:, rows],
                rhs=w_codes["u3"][:].bitcast(FP8X4), rhs_scale=w_scales["u3"][:],
                start=False, stop=True,
            )
            cand_bank[i] = bank

        def add_bias(i):
            g, j = divmod(i, GROUP_TILES)
            nc.vector.tensor_tensor(out=results[g][:, j, :], in0=cand_bank[i][:], in1=bias_rows[:], op=ALU.add)

        def finish(i):
            g, j = divmod(i, GROUP_TILES)
            result = results[g]
            nc.scalar.activation(out=result[:, j, :], in_=result[:, j, :], func=ACT.Tanh)
            nc.sync.dma_start(out=out_rows[:, i:i + 1, :], in_=result[:, j:j + 1, :])

        first_sigmoid = keep.tile([P, 1], F32, name="first_sigmoid")
        nc.vector.memset(first_sigmoid[:], 0.0)
        nc.scalar.activation(out=first_sigmoid[:], in_=first_sigmoid[:], func=ACT.Sigmoid)

        bias_gate_bf = keep.tile([P, CHUNKS], BF16, name="bias_gate_bf")
        nc.scalar.dma_start(out=bias_gate_bf[:], in_=bias_r.rearrange("o (q t) -> q (o t)", t=CHUNKS))
        bias_row = keep.tile([P, FEAT], BF16, name="bias_row")
        nc.gpsimd.memset(bias_row[:], 0.0)
        nc.scalar.dma_start(out=bias_row[0:1, :], in_=bias_u)
        identity = keep.tile([P, P], F32, name="identity")
        make_identity(nc, identity[:])
        ones = keep.tile([P, P], BF16, name="ones")
        nc.gpsimd.memset(ones[:], 1.0)
        bias_rows = keep.tile([P, FEAT], F32, name="bias_rows")

        load_weight("w1", w1)
        load_rows("x", 0, pieces=2)
        load_rows("h", 0, pieces=2)
        load_weight("u1", u1)
        load_rows("x", 1, pieces=1)
        load_rows("h", 1, pieces=1)
        load_weight("w3", w3)
        load_rows("x", 2, pieces=1)
        load_rows("h", 2, pieces=1)
        load_weight("u3", u3)
        load_rows("x", 3, pieces=1)
        load_rows("h", 3, pieces=1)
        load_rows("x", 4, pieces=1)
        load_rows("h", 4, pieces=1)

        zeros = keep.tile([P, FEAT], BF16, name="zeros")
        nc.vector.memset(zeros[:], 0.0)

        def keep_clock(name, matmuls):
            bank = psum["gate"].tile([P, FEAT], F32, name=name, tag="gate")
            for i in range(matmuls):
                nc.tensor.matmul(out=bank[:], lhsT=zeros[:, :P], rhs=zeros[:], start=True, stop=True)

        keep_clock("unread_a", 7)
        transpose_rows("x", 0)
        regroup_weight("w1", stationary=True)
        bias_gate = keep.tile([P, CHUNKS], F32, name="bias_gate")
        nc.vector.tensor_copy(out=bias_gate[:], in_=bias_gate_bf[:])
        quantise_weight("w1", pieces=1)
        quantise_rows("x", 0)
        keep_clock("unread_b", 2)
        transpose_rows("h", 0)
        for t in range(3):
            gate_pass(0, t, "w1", "x")
        regroup_weight("u1", stationary=True)
        quantise_rows("h", 0)
        quantise_weight("u1", pieces=1)
        for key in ("x", "h"):
            transpose_rows(key, 1)
            quantise_rows(key, 1)

        filled = 0
        finished = 0
        state_waits = None
        for n in range(GROUPS):
            for half in range(2):
                ready = filled
                fill = half < FILLS[n]
                gate(n, (2 * half, 2 * half + 1))
                if n == 0 and half == 1:
                    bank = psum["candidate"].tile([P, FEAT], F32, name="bias_bank", tag="candidate")
                    nc.tensor.matmul(out=bank[:], lhsT=ones[:], rhs=bias_row[:], start=True, stop=True)
                    nc.scalar.copy(out=bias_rows[:], in_=bank[:])
                    regroup_weight("w3", stationary=False)
                    regroup_weight("u3", stationary=False)
                    quantise_weight("w3", pieces=1)
                    quantise_weight("u3", pieces=1)
                if 1 <= n <= ON_GPSIMD:
                    if half == 0:
                        reset_state(n - 1, nc.vector, 0, 1)
                elif n > ON_GPSIMD:
                    for j in range(2 * half, 2 * half + 2):
                        reset_state(n - 1, nc.gpsimd, j, GROUP_TILES)
                if fill:
                    candidate_sum(filled, "candidate")
                    filled += 1
                while finished < ready:
                    finish(finished)
                    finished += 1
                if n + LEAD < GROUPS:
                    transpose_rows(("x", "h")[half], n + LEAD)
                if half == 0 and state_waits is not None:
                    quantise_rows("h", state_waits)
                    state_waits = None
                if half == 1:
                    if n + LEAD < GROUPS:
                        quantise_rows("x", n + LEAD)
                        state_waits = n + LEAD
                    if 1 <= n <= ON_GPSIMD:
                        quantise_reset_state(n - 1)
                if fill:
                    add_bias(filled - 1)

        for j in range(GROUP_TILES):
            reset_state(GROUPS - 1, nc.gpsimd, j, GROUP_TILES)
        for i in range(filled, TILES):
            if i % GROUP_TILES == 2 and ON_GPSIMD <= i // GROUP_TILES + 1 < GROUPS:
                quantise_reset_state(i // GROUP_TILES + 1)
            candidate_sum(i, TURNS[(i - filled) % len(TURNS)])
            add_bias(i)
            finish(i - 1)
        finish(TILES - 1)
